import numpy as np
import ml_dtypes


def mxq(x, axis, fmt="e4m3"):
    dtype, down = {"e4m3": (ml_dtypes.float8_e4m3fn, 7), "e5m2": (ml_dtypes.float8_e5m2, 14)}[fmt]
    v = np.moveaxis(np.asarray(x, np.float32).astype(ml_dtypes.bfloat16).astype(np.float64), axis, -1)
    blocks = v.reshape(v.shape[:-1] + (-1, 32))
    amax = np.abs(blocks).max(-1, keepdims=True)
    byte = np.maximum(np.where(amax > 0, np.frexp(amax)[1] - 1 + 127, 0) - down, 1)
    scale = np.exp2(byte - 127.0)
    codes = (blocks / scale).astype(np.float32).astype(dtype).astype(np.float64)
    return np.moveaxis((codes * scale).reshape(v.shape), -1, axis)


WIDE = False


def mx_kscale(k):
    if not WIDE:
        return np.ones(k)
    levels = np.array([10, -10, 5, -5, 0])
    a = np.random.permutation(np.resize(levels, k // 512 * 4)).reshape(k // 512, 4)
    idx = np.arange(k)
    return np.exp2(a[idx // 512, idx % 128 // 32])


BF16 = ml_dtypes.bfloat16


def bf(x):
    return np.asarray(x, np.float32).astype(BF16)


def f64(x):
    return np.asarray(x).astype(np.float64)


W, M, K, N = 4, 256, 512, 256


def setup_inputs():
    s = mx_kscale(K)
    return {"x": bf(np.random.standard_normal((W, M, K)) * s),
            "weight": bf(np.random.standard_normal((W, N, K)) / np.sqrt(W * K) / s),
            "bias": bf(np.random.standard_normal((W, M, N)) / np.sqrt(W))}


def reference(x, weight, bias):
    w, m, _ = x.shape
    xq = mxq(f64(x), 2, "e4m3")
    wq = mxq(f64(weight), 2, "e4m3")
    y = (xq @ wq.transpose(0, 2, 1)).sum(0) + f64(bias).sum(0)
    m_per_rank = m // w
    return y.reshape(w, m_per_rank, -1)

@@ -1,0 +1,137 @@
+from contextlib import ExitStack
+
+import concourse.mybir as mybir
+from concourse.masks import make_identity
+
+BF16 = mybir.dt.bfloat16
+F32 = mybir.dt.float32
+U32 = mybir.dt.uint32
+U8 = mybir.dt.uint8
+FP8X4 = mybir.dt.float8_e4m3fn_x4
+ADD = mybir.AluOpType.add
+
+P = 128
+RANKS = 4
+M = 256
+N = 256
+K = 512
+PARITIES = 2
+PACK = 4
+PLANES = 2
+ROW_WORDS = K // 2
+BIAS_AFTER_RANK = 1
+
+FLOPS = 2 * M * N * K * RANKS
+
+
+def flip(nc, psum, tag, identity, words, grouped):
+    rows = words.shape[1] // ROW_WORDS
+    flipped = psum.tile([P, rows, PLANES, P], F32, tag=tag)
+    for g in range(rows):
+        for u in range(PLANES):
+            first = (g * PLANES + u) * P
+            nc.tensor.transpose(flipped[:, g, u, :], words[:, first : first + P], identity[:])
+    nc.scalar.copy(
+        out=grouped[:].bitcast(F32).rearrange("p (g c u) -> p g c u", g=rows, u=PLANES),
+        in_=flipped[:].rearrange("p g u c -> p g c u"),
+    )
+
+
+def tile_gemmrstritonpcie_s_kernel(tc, x, weight, bias, out):
+    nc = tc.nc
+    with ExitStack() as ctx:
+        ctx.enter_context(tc.manual_schedule())
+        keep = ctx.enter_context(tc.tile_pool(name="keep", bufs=1))
+        psum_w = ctx.enter_context(tc.psum_pool(name="psum_w", bufs=2))
+        psum_x = ctx.enter_context(tc.psum_pool(name="psum_x", bufs=2 * PARITIES))
+        sums = ctx.enter_context(tc.psum_pool(name="sums", bufs=1))
+
+        w_rows = []
+        x_rows = []
+        bias_rows = keep.tile([P, RANKS, PARITIES * N], BF16)
+        for r in range(RANKS):
+            w_rows.append(keep.tile([P, PARITIES * K], BF16, name="w_rows%d" % r))
+            x_rows.append(keep.tile([P, PARITIES * K], BF16, name="x_rows%d" % r))
+            nc.sync.dma_start(
+                out=w_rows[r][:], in_=weight[r].rearrange("(p s) k -> p (s k)", s=PARITIES)
+            )
+            nc.sync.dma_start(
+                out=x_rows[r][:], in_=x[r].rearrange("(p s) k -> p (s k)", s=PARITIES)
+            )
+            if r == BIAS_AFTER_RANK:
+                nc.sync.dma_start(
+                    out=bias_rows[:], in_=bias.rearrange("r (p s) n -> p r (s n)", s=PARITIES)
+                )
+
+        identity = keep.tile([P, P], F32)
+        make_identity(nc, identity[:])
+
+        acc = [sums.tile([P, N], F32, name="acc%d" % s) for s in range(PARITIES)]
+        w_codes = [keep.tile([P, N], U32, name="w_codes%d" % r, align_bytes=64) for r in range(RANKS)]
+        w_scales = [keep.tile([P, N], U8, name="w_scales%d" % r, align_bytes=64) for r in range(RANKS)]
+        x_codes = [keep.tile([P, M], U32, name="x_codes%d" % r, align_bytes=64) for r in range(RANKS)]
+        x_scales = [keep.tile([P, M], U8, name="x_scales%d" % r, align_bytes=64) for r in range(RANKS)]
+
+        def multiply(r, s):
+            m_cols = slice(s * P, (s + 1) * P)
+            nc.tensor.matmul_mx(
+                out=acc[s][:],
+                lhsT=x_codes[r][:, m_cols].bitcast(FP8X4),
+                lhsT_scale=x_scales[r][:, m_cols],
+                rhs=w_codes[r][:].bitcast(FP8X4),
+                rhs_scale=w_scales[r][:],
+                start=(r == 0),
+                stop=(r == RANKS - 1),
+            )
+
+        for r in range(RANKS):
+            w_grouped = keep.tile([P, N * PACK], BF16, name="w_grouped%d" % r, align_bytes=64)
+            flip(nc, psum_w, "w_flipped", identity, w_rows[r][:].bitcast(F32), w_grouped)
+            x_grouped = []
+            for s in range(PARITIES):
+                x_grouped.append(
+                    keep.tile([P, P * PACK], BF16, name="x_grouped%d_%d" % (r, s), align_bytes=64)
+                )
+                words = x_rows[r][:].bitcast(F32)[:, s * ROW_WORDS : (s + 1) * ROW_WORDS]
+                flip(nc, psum_x, "x_flipped", identity, words, x_grouped[s])
+
+            if r > 0:
+                for s in range(PARITIES):
+                    multiply(r - 1, s)
+
+            nc.vector.quantize_mx(
+                out=w_codes[r][:].bitcast(FP8X4), scales=w_scales[r][:], in_=w_grouped[:]
+            )
+            for s in range(PARITIES):
+                m_cols = slice(s * P, (s + 1) * P)
+                nc.vector.quantize_mx(
+                    out=x_codes[r][:, m_cols].bitcast(FP8X4),
+                    scales=x_scales[r][:, m_cols],
+                    in_=x_grouped[s][:],
+                )
+
+            if r == BIAS_AFTER_RANK:
+                bias_pairs = keep.tile([P, 2, PARITIES * N], F32)
+                bias_sum = keep.tile([P, PARITIES, N], F32)
+                nc.vector.tensor_tensor(
+                    out=bias_pairs[:], in0=bias_rows[:, 0:2, :], in1=bias_rows[:, 2:4, :], op=ADD
+                )
+                nc.vector.tensor_tensor(
+                    out=bias_sum[:].rearrange("p s n -> p (s n)"),
+                    in0=bias_pairs[:, 0, :],
+                    in1=bias_pairs[:, 1, :],
+                    op=ADD,
+                )
+
+        y_rows = out.rearrange("r q n -> (r q) n").rearrange("(p s) n -> p s n", s=PARITIES)
+        for s in range(PARITIES):
+            multiply(RANKS - 1, s)
+        for s in range(PARITIES):
+            y = keep.tile([P, N], F32, name="y%d" % s)
+            nc.vector.tensor_tensor(
+                out=y[:].rearrange("p (c t) -> p c t", t=PARITIES),
+                in0=acc[s][:].rearrange("p (t c) -> p c t", t=PARITIES),
+                in1=bias_sum[:, s, :].rearrange("p (c t) -> p c t", t=PARITIES),
+                op=ADD,
+            )
+            nc.sync.dma_start(out=y_rows[:, s, :], in_=y[:])

@@ -95,10 +95,6 @@ def tile_gemmrstritonpcie_s_kernel(tc, x, weight, bias, out):
                 words = x_rows[r][:].bitcast(F32)[:, s * ROW_WORDS : (s + 1) * ROW_WORDS]
                 flip(nc, psum_x, "x_flipped", identity, words, x_grouped[s])
 
-            if r > 0:
-                for s in range(PARITIES):
-                    multiply(r - 1, s)
-
             nc.vector.quantize_mx(
                 out=w_codes[r][:].bitcast(FP8X4), scales=w_scales[r][:], in_=w_grouped[:]
             )
@@ -124,8 +120,9 @@ def tile_gemmrstritonpcie_s_kernel(tc, x, weight, bias, out):
                 )
 
         y_rows = out.rearrange("r q n -> (r q) n").rearrange("(p s) n -> p s n", s=PARITIES)
-        for s in range(PARITIES):
-            multiply(RANKS - 1, s)
+        for r in range(RANKS):
+            for s in range(PARITIES):
+                multiply(r, s)
         for s in range(PARITIES):
             y = keep.tile([P, N], F32, name="y%d" % s)
             nc.vector.tensor_tensor(

@@ -19,6 +19,7 @@ PARITIES = 2
 PACK = 4
 PLANES = 2
 ROW_WORDS = K // 2
+BANKS = 8
 BIAS_AFTER_RANK = 1
 
 FLOPS = 2 * M * N * K * RANKS
@@ -42,9 +43,13 @@ def tile_gemmrstritonpcie_s_kernel(tc, x, weight, bias, out):
     with ExitStack() as ctx:
         ctx.enter_context(tc.manual_schedule())
         keep = ctx.enter_context(tc.tile_pool(name="keep", bufs=1))
-        psum_w = ctx.enter_context(tc.psum_pool(name="psum_w", bufs=2))
-        psum_x = ctx.enter_context(tc.psum_pool(name="psum_x", bufs=2 * PARITIES))
+        psum = ctx.enter_context(tc.psum_pool(name="psum", bufs=BANKS - PARITIES))
         sums = ctx.enter_context(tc.psum_pool(name="sums", bufs=1))
+
+        def x_pieces(r):
+            if r == RANKS - 1:
+                return [(s, s + 1) for s in range(PARITIES)]
+            return [(0, PARITIES)]
 
         w_rows = []
         x_rows = []
@@ -55,9 +60,11 @@ def tile_gemmrstritonpcie_s_kernel(tc, x, weight, bias, out):
             nc.sync.dma_start(
                 out=w_rows[r][:], in_=weight[r].rearrange("(p s) k -> p (s k)", s=PARITIES)
             )
-            nc.sync.dma_start(
-                out=x_rows[r][:], in_=x[r].rearrange("(p s) k -> p (s k)", s=PARITIES)
-            )
+            for first, end in x_pieces(r):
+                nc.sync.dma_start(
+                    out=x_rows[r][:].rearrange("p (s k) -> p s k", s=PARITIES)[:, first:end, :],
+                    in_=x[r].rearrange("(p s) k -> p s k", s=PARITIES)[:, first:end, :],
+                )
             if r == BIAS_AFTER_RANK:
                 nc.sync.dma_start(
                     out=bias_rows[:], in_=bias.rearrange("r (p s) n -> p r (s n)", s=PARITIES)
@@ -72,43 +79,51 @@ def tile_gemmrstritonpcie_s_kernel(tc, x, weight, bias, out):
         x_codes = [keep.tile([P, M], U32, name="x_codes%d" % r, align_bytes=64) for r in range(RANKS)]
         x_scales = [keep.tile([P, M], U8, name="x_scales%d" % r, align_bytes=64) for r in range(RANKS)]
 
-        def multiply(r, s):
-            m_cols = slice(s * P, (s + 1) * P)
-            nc.tensor.matmul_mx(
-                out=acc[s][:],
-                lhsT=x_codes[r][:, m_cols].bitcast(FP8X4),
-                lhsT_scale=x_scales[r][:, m_cols],
-                rhs=w_codes[r][:].bitcast(FP8X4),
-                rhs_scale=w_scales[r][:],
-                start=(r == 0),
-                stop=(r == RANKS - 1),
-            )
-
-        for r in range(RANKS):
+        def quantise_rank(r):
             w_grouped = keep.tile([P, N * PACK], BF16, name="w_grouped%d" % r, align_bytes=64)
-            flip(nc, psum_w, "w_flipped", identity, w_rows[r][:].bitcast(F32), w_grouped)
+            flip(nc, psum, "flipped", identity, w_rows[r][:].bitcast(F32), w_grouped)
             x_grouped = []
-            for s in range(PARITIES):
+            for first, end in x_pieces(r):
                 x_grouped.append(
-                    keep.tile([P, P * PACK], BF16, name="x_grouped%d_%d" % (r, s), align_bytes=64)
+                    keep.tile(
+                        [P, (end - first) * P * PACK],
+                        BF16,
+                        name="x_grouped%d_%d" % (r, first),
+                        align_bytes=64,
+                    )
                 )
-                words = x_rows[r][:].bitcast(F32)[:, s * ROW_WORDS : (s + 1) * ROW_WORDS]
-                flip(nc, psum_x, "x_flipped", identity, words, x_grouped[s])
+                words = x_rows[r][:].bitcast(F32)[:, first * ROW_WORDS : end * ROW_WORDS]
+                flip(nc, psum, "flipped", identity, words, x_grouped[-1])
 
             nc.vector.quantize_mx(
                 out=w_codes[r][:].bitcast(FP8X4), scales=w_scales[r][:], in_=w_grouped[:]
             )
-            for s in range(PARITIES):
-                m_cols = slice(s * P, (s + 1) * P)
+            for (first, end), grouped in zip(x_pieces(r), x_grouped):
+                m_cols = slice(first * P, end * P)
                 nc.vector.quantize_mx(
                     out=x_codes[r][:, m_cols].bitcast(FP8X4),
                     scales=x_scales[r][:, m_cols],
-                    in_=x_grouped[s][:],
+                    in_=grouped[:],
                 )
 
+        def multiply_rank(r):
+            for s in range(PARITIES):
+                m_cols = slice(s * P, (s + 1) * P)
+                nc.tensor.matmul_mx(
+                    out=acc[s][:],
+                    lhsT=x_codes[r][:, m_cols].bitcast(FP8X4),
+                    lhsT_scale=x_scales[r][:, m_cols],
+                    rhs=w_codes[r][:].bitcast(FP8X4),
+                    rhs_scale=w_scales[r][:],
+                    start=(r == 0),
+                    stop=(r == RANKS - 1),
+                )
+
+        bias_pairs = keep.tile([P, 2, PARITIES * N], F32)
+        bias_sum = keep.tile([P, PARITIES, N], F32)
+        for r in range(RANKS):
+            quantise_rank(r)
             if r == BIAS_AFTER_RANK:
-                bias_pairs = keep.tile([P, 2, PARITIES * N], F32)
-                bias_sum = keep.tile([P, PARITIES, N], F32)
                 nc.vector.tensor_tensor(
                     out=bias_pairs[:], in0=bias_rows[:, 0:2, :], in1=bias_rows[:, 2:4, :], op=ADD
                 )
@@ -118,11 +133,12 @@ def tile_gemmrstritonpcie_s_kernel(tc, x, weight, bias, out):
                     in1=bias_pairs[:, 1, :],
                     op=ADD,
                 )
+                for earlier in range(BIAS_AFTER_RANK):
+                    multiply_rank(earlier)
+        for r in range(BIAS_AFTER_RANK, RANKS):
+            multiply_rank(r)
 
         y_rows = out.rearrange("r q n -> (r q) n").rearrange("(p s) n -> p s n", s=PARITIES)
-        for r in range(RANKS):
-            for s in range(PARITIES):
-                multiply(r, s)
         for s in range(PARITIES):
             y = keep.tile([P, N], F32, name="y%d" % s)
             nc.vector.tensor_tensor(

from contextlib import ExitStack

import concourse.mybir as mybir
from concourse.masks import make_identity

BF16 = mybir.dt.bfloat16
F32 = mybir.dt.float32
U32 = mybir.dt.uint32
U8 = mybir.dt.uint8
FP8X4 = mybir.dt.float8_e4m3fn_x4
ADD = mybir.AluOpType.add

P = 128
RANKS = 4
M = 256
N = 256
K = 512
PARITIES = 2
PACK = 4
PLANES = 2
ROW_WORDS = K // 2
BANKS = 8
BIAS_AFTER_RANK = 1

FLOPS = 2 * M * N * K * RANKS


def flip(nc, psum, tag, identity, words, grouped):
    rows = words.shape[1] // ROW_WORDS
    flipped = psum.tile([P, rows, PLANES, P], F32, tag=tag)
    for g in range(rows):
        for u in range(PLANES):
            first = (g * PLANES + u) * P
            nc.tensor.transpose(flipped[:, g, u, :], words[:, first : first + P], identity[:])
    nc.scalar.copy(
        out=grouped[:].bitcast(F32).rearrange("p (g c u) -> p g c u", g=rows, u=PLANES),
        in_=flipped[:].rearrange("p g u c -> p g c u"),
    )


def tile_gemmrstritonpcie_s_kernel(tc, x, weight, bias, out):
    nc = tc.nc
    with ExitStack() as ctx:
        ctx.enter_context(tc.manual_schedule())
        keep = ctx.enter_context(tc.tile_pool(name="keep", bufs=1))
        psum = ctx.enter_context(tc.psum_pool(name="psum", bufs=BANKS - PARITIES))
        sums = ctx.enter_context(tc.psum_pool(name="sums", bufs=1))

        def x_pieces(r):
            if r == RANKS - 1:
                return [(s, s + 1) for s in range(PARITIES)]
            return [(0, PARITIES)]

        w_rows = []
        x_rows = []
        bias_rows = keep.tile([P, RANKS, PARITIES * N], BF16)
        for r in range(RANKS):
            w_rows.append(keep.tile([P, PARITIES * K], BF16, name="w_rows%d" % r))
            x_rows.append(keep.tile([P, PARITIES * K], BF16, name="x_rows%d" % r))
            nc.sync.dma_start(
                out=w_rows[r][:], in_=weight[r].rearrange("(p s) k -> p (s k)", s=PARITIES)
            )
            for first, end in x_pieces(r):
                nc.sync.dma_start(
                    out=x_rows[r][:].rearrange("p (s k) -> p s k", s=PARITIES)[:, first:end, :],
                    in_=x[r].rearrange("(p s) k -> p s k", s=PARITIES)[:, first:end, :],
                )
            if r == BIAS_AFTER_RANK:
                nc.sync.dma_start(
                    out=bias_rows[:], in_=bias.rearrange("r (p s) n -> p r (s n)", s=PARITIES)
                )

        identity = keep.tile([P, P], F32)
        make_identity(nc, identity[:])

        acc = [sums.tile([P, N], F32, name="acc%d" % s) for s in range(PARITIES)]
        w_codes = [keep.tile([P, N], U32, name="w_codes%d" % r, align_bytes=64) for r in range(RANKS)]
        w_scales = [keep.tile([P, N], U8, name="w_scales%d" % r, align_bytes=64) for r in range(RANKS)]
        x_codes = [keep.tile([P, M], U32, name="x_codes%d" % r, align_bytes=64) for r in range(RANKS)]
        x_scales = [keep.tile([P, M], U8, name="x_scales%d" % r, align_bytes=64) for r in range(RANKS)]

        def quantise_rank(r):
            w_grouped = keep.tile([P, N * PACK], BF16, name="w_grouped%d" % r, align_bytes=64)
            flip(nc, psum, "flipped", identity, w_rows[r][:].bitcast(F32), w_grouped)
            x_grouped = []
            for first, end in x_pieces(r):
                x_grouped.append(
                    keep.tile(
                        [P, (end - first) * P * PACK],
                        BF16,
                        name="x_grouped%d_%d" % (r, first),
                        align_bytes=64,
                    )
                )
                words = x_rows[r][:].bitcast(F32)[:, first * ROW_WORDS : end * ROW_WORDS]
                flip(nc, psum, "flipped", identity, words, x_grouped[-1])

            nc.vector.quantize_mx(
                out=w_codes[r][:].bitcast(FP8X4), scales=w_scales[r][:], in_=w_grouped[:]
            )
            for (first, end), grouped in zip(x_pieces(r), x_grouped):
                m_cols = slice(first * P, end * P)
                nc.vector.quantize_mx(
                    out=x_codes[r][:, m_cols].bitcast(FP8X4),
                    scales=x_scales[r][:, m_cols],
                    in_=grouped[:],
                )

        def multiply_rank(r):
            for s in range(PARITIES):
                m_cols = slice(s * P, (s + 1) * P)
                nc.tensor.matmul_mx(
                    out=acc[s][:],
                    lhsT=x_codes[r][:, m_cols].bitcast(FP8X4),
                    lhsT_scale=x_scales[r][:, m_cols],
                    rhs=w_codes[r][:].bitcast(FP8X4),
                    rhs_scale=w_scales[r][:],
                    start=(r == 0),
                    stop=(r == RANKS - 1),
                )

        bias_pairs = keep.tile([P, 2, PARITIES * N], F32)
        bias_sum = keep.tile([P, PARITIES, N], F32)
        for r in range(RANKS):
            quantise_rank(r)
            if r == BIAS_AFTER_RANK:
                nc.vector.tensor_tensor(
                    out=bias_pairs[:], in0=bias_rows[:, 0:2, :], in1=bias_rows[:, 2:4, :], op=ADD
                )
                nc.vector.tensor_tensor(
                    out=bias_sum[:].rearrange("p s n -> p (s n)"),
                    in0=bias_pairs[:, 0, :],
                    in1=bias_pairs[:, 1, :],
                    op=ADD,
                )
                for earlier in range(BIAS_AFTER_RANK):
                    multiply_rank(earlier)
        for r in range(BIAS_AFTER_RANK, RANKS):
            multiply_rank(r)

        y_rows = out.rearrange("r q n -> (r q) n").rearrange("(p s) n -> p s n", s=PARITIES)
        for s in range(PARITIES):
            y = keep.tile([P, N], F32, name="y%d" % s)
            nc.vector.tensor_tensor(
                out=y[:].rearrange("p (c t) -> p c t", t=PARITIES),
                in0=acc[s][:].rearrange("p (t c) -> p c t", t=PARITIES),
                in1=bias_sum[:, s, :].rearrange("p (c t) -> p c t", t=PARITIES),
                op=ADD,
            )
            nc.sync.dma_start(out=y_rows[:, s, :], in_=y[:])
